import numpy as np
import ml_dtypes


def mxq(x, axis, fmt="e4m3"):
    dtype, down = {"e4m3": (ml_dtypes.float8_e4m3fn, 7), "e5m2": (ml_dtypes.float8_e5m2, 14)}[fmt]
    v = np.moveaxis(np.asarray(x, np.float32).astype(ml_dtypes.bfloat16).astype(np.float64), axis, -1)
    blocks = v.reshape(v.shape[:-1] + (-1, 32))
    amax = np.abs(blocks).max(-1, keepdims=True)
    byte = np.maximum(np.where(amax > 0, np.frexp(amax)[1] - 1 + 127, 0) - down, 1)
    scale = np.exp2(byte - 127.0)
    codes = (blocks / scale).astype(np.float32).astype(dtype).astype(np.float64)
    return np.moveaxis((codes * scale).reshape(v.shape), -1, axis)


WIDE = False


def mx_kscale(k):
    if not WIDE:
        return np.ones(k)
    levels = np.array([10, -10, 5, -5, 0])
    a = np.random.permutation(np.resize(levels, k // 512 * 4)).reshape(k // 512, 4)
    idx = np.arange(k)
    return np.exp2(a[idx // 512, idx % 128 // 32])


BF16 = ml_dtypes.bfloat16


def bf(x):
    return np.asarray(x, np.float32).astype(BF16)


def f64(x):
    return np.asarray(x).astype(np.float64)


B, S, D, H, QL, KL, ND, VD, RD = 4, 1024, 1024, 4, 512, 512, 64, 64, 128
BASE = 10000.0


def rope(v):
    d = v.shape[-1]
    inv_freq = BASE ** (-np.arange(0, d, 2) / d)
    ang = np.arange(v.shape[1])[:, None] * inv_freq[None, :]
    cos = np.cos(ang)[None, :, None, :]
    sin = np.sin(ang)[None, :, None, :]
    v1 = v[..., 0::2]
    v2 = v[..., 1::2]
    o1 = v1 * cos - v2 * sin
    o2 = v1 * sin + v2 * cos
    return np.stack([o1, o2], axis=-1).reshape(v.shape)


def setup_inputs():
    s, t = mx_kscale(D), mx_kscale(KL)
    tc = np.concatenate([t, np.ones(RD)])
    return {"x": bf(np.random.standard_normal((B, S, D)) * s),
            "Wkva": bf(np.random.standard_normal((D, KL + RD)) / np.sqrt(D) / s[:, None] * tc),
            "Wkvb": bf(np.random.standard_normal((KL, H * (ND + VD))) / np.sqrt(KL) / t[:, None])}


def reference(x, Wkva, Wkvb):
    ckv = mxq(f64(x), 2, "e4m3") @ mxq(f64(Wkva), 0, "e4m3")
    compressed_kv, k_pe = ckv[..., :KL], ckv[..., KL:]
    k_pe = np.broadcast_to(k_pe[:, :, None, :], (B, S, H, RD))
    kv = (mxq(compressed_kv, 2, "e4m3") @ mxq(f64(Wkvb), 0, "e4m3")).reshape(B, S, H, ND + VD)
    k_nope, v = kv[..., :ND], kv[..., ND:]
    kf = np.concatenate([k_nope, rope(k_pe)], axis=-1)
    return kf, v

@@ -1,0 +1,335 @@
+import math
+from contextlib import ExitStack
+
+import concourse.mybir as mybir
+from concourse.masks import make_identity
+
+F32 = mybir.dt.float32
+BF16 = mybir.dt.bfloat16
+I32 = mybir.dt.int32
+U32 = mybir.dt.uint32
+U8 = mybir.dt.uint8
+FP8X4 = mybir.dt.float8_e4m3fn_x4
+ALU = mybir.AluOpType
+ACT = mybir.ActivationFunctionType
+
+P = 128
+PACK = 4
+TOKENS = 4 * 1024
+SEQ = 1024
+D = 1024
+PASSES = D // (P * PACK)
+KL = 512
+RD = 128
+PAIRS = RD // 2
+H = 4
+ND = 64
+VD = 64
+CKV = KL + RD
+ROPE_BASE = 10000.0
+
+TILES = 2
+UNIT = TILES * P
+UNITS = TOKENS // UNIT
+PHASES = SEQ // UNIT
+
+ROUND_MAGIC = 1.5 * 2.0**23
+
+FLOPS = 2 * TOKENS * D * CKV + 2 * TOKENS * KL * H * (ND + VD)
+
+
+def tile_multilatentattention_pb_t_kernel(tc, x, Wkva, Wkvb, out_0, out_1):
+    nc = tc.nc
+    x_units = x.flatten_outer_dims().rearrange("(n p i) k -> n p (i k)", p=P, i=TILES)
+    kf_units = out_0.rearrange("b s h f -> (b s) (h f)").rearrange(
+        "(n p i) f -> n p (i f)", p=P, i=TILES
+    )
+    v_units = out_1.rearrange("b s h f -> (b s) (h f)").rearrange(
+        "(n p i) f -> n p (i f)", p=P, i=TILES
+    )
+
+    with ExitStack() as ctx:
+        keep = ctx.enter_context(tc.tile_pool(name="keep", bufs=1))
+        x_pool = ctx.enter_context(tc.tile_pool(name="x_pool", bufs=UNITS))
+        stage = ctx.enter_context(tc.tile_pool(name="stage", bufs=2))
+        codes = ctx.enter_context(tc.tile_pool(name="codes", bufs=3))
+        results = ctx.enter_context(tc.tile_pool(name="results", bufs=4))
+        xt_banks = ctx.enter_context(tc.psum_pool(name="xt_banks", bufs=2))
+        c_banks = ctx.enter_context(tc.psum_pool(name="c_banks", bufs=2))
+        kv_banks = ctx.enter_context(tc.psum_pool(name="kv_banks", bufs=2))
+        pe_banks = ctx.enter_context(tc.psum_pool(name="pe_banks", bufs=2))
+        ctx.enter_context(tc.manual_schedule())
+
+        wa_rows = Wkva.rearrange("(g u q e) c -> g q u (e c)", g=PASSES, u=2, q=P, e=2)
+        wa_raw = keep.tile([P, PASSES, PACK, CKV], BF16)
+        x_sb = {}
+
+        def load_x(n):
+            x_sb[n] = x_pool.tile([P, TILES * D], BF16, name="x_sb")
+            nc.sync.dma_start(out=x_sb[n][:], in_=x_units[n])
+
+        for g in range(PASSES):
+            nc.sync.dma_start(
+                out=wa_raw[:, g].rearrange("q (u e) c -> q u (e c)", u=2), in_=wa_rows[g]
+            )
+        load_x(0)
+        wb_raw = keep.tile([P, PACK, H * (ND + VD)], BF16)
+        nc.sync.dma_start(out=wb_raw[:], in_=Wkvb.rearrange("(m q) n -> q m n", q=P))
+        for n in range(1, UNITS):
+            load_x(n)
+
+        ident = keep.tile([P, P], F32)
+        make_identity(nc, ident[:])
+
+        warm = keep.tile([P, 1], F32)
+        nc.vector.memset(warm[:], 0.0)
+        nc.scalar.activation(out=warm[:], in_=warm[:], func=ACT.Sin)
+        pos_i = keep.tile([P, PHASES * TILES], I32)
+        nc.gpsimd.iota(
+            pos_i[:], pattern=[[UNIT, PHASES], [1, TILES]], base=0, channel_multiplier=TILES
+        )
+        pos = keep.tile([P, PHASES * TILES], F32)
+        nc.vector.tensor_copy(out=pos[:], in_=pos_i[:])
+        turns = keep.tile([P, PAIRS], F32)
+        nc.vector.memset(turns[:, 0:1], 1.0)
+        nc.vector.tensor_scalar_mul(out=turns[:, 0:1], in0=turns[:, 0:1], scalar1=0.5 / math.pi)
+        filled = 1
+        while filled < PAIRS:
+            nc.vector.tensor_scalar_mul(
+                out=turns[:, filled : 2 * filled],
+                in0=turns[:, 0:filled],
+                scalar1=ROPE_BASE ** (-2.0 * filled / RD),
+            )
+            filled *= 2
+        table_shape = [P, PHASES * TILES, PAIRS]
+        angle = keep.tile(table_shape, F32)
+        nc.vector.tensor_tensor(
+            out=angle[:],
+            in0=pos[:].unsqueeze(2).to_broadcast(table_shape),
+            in1=turns[:].unsqueeze(1).to_broadcast(table_shape),
+            op=ALU.mult,
+        )
+        whole = keep.tile(table_shape, F32)
+        nc.vector.tensor_scalar(
+            out=whole[:],
+            in0=angle[:],
+            scalar1=ROUND_MAGIC,
+            scalar2=ROUND_MAGIC,
+            op0=ALU.add,
+            op1=ALU.subtract,
+        )
+        frac = keep.tile(table_shape, F32)
+        nc.vector.tensor_sub(out=frac[:], in0=angle[:], in1=whole[:])
+        frac_abs = keep.tile(table_shape, F32)
+        nc.vector.scalar_tensor_tensor(
+            out=frac_abs[:], in0=frac[:], scalar=-1.0, in1=frac[:], op0=ALU.mult, op1=ALU.max
+        )
+        quarter_off = keep.tile(table_shape, F32)
+        nc.vector.tensor_scalar(
+            out=quarter_off[:],
+            in0=frac_abs[:],
+            scalar1=-1.0,
+            scalar2=0.25,
+            op0=ALU.mult,
+            op1=ALU.add,
+        )
+        sin_t = keep.tile(table_shape, F32)
+        cos_t = keep.tile(table_shape, F32)
+        nc.scalar.activation(out=sin_t[:], in_=frac[:], func=ACT.Sin, scale=2.0 * math.pi)
+        nc.scalar.activation(out=cos_t[:], in_=quarter_off[:], func=ACT.Sin, scale=2.0 * math.pi)
+
+        wa_grouped = keep.tile([P, PASSES, CKV, PACK], BF16, align_bytes=64)
+        wa_codes = keep.tile([P, PASSES, CKV], U32, align_bytes=64)
+        wa_scales = keep.tile([P, PASSES, CKV], U8, align_bytes=64)
+        for g in range(PASSES):
+            nc.vector.tensor_copy(
+                out=wa_grouped[:, g, 0:KL, :],
+                in_=wa_raw[:, g, :, 0:KL].rearrange("q t c -> q c t"),
+            )
+            nc.scalar.copy(
+                out=wa_grouped[:, g, KL:CKV, :].rearrange("q (e j) t -> q e j t", e=2),
+                in_=wa_raw[:, g, :, KL:CKV].rearrange("q t (j e) -> q e j t", e=2),
+            )
+        for g in range(PASSES):
+            for cols in (slice(0, KL), slice(KL, CKV)):
+                nc.vector.quantize_mx(
+                    out=wa_codes[:, g, cols].bitcast(FP8X4),
+                    scales=wa_scales[:, g, cols],
+                    in_=wa_grouped[:, g, cols, :].rearrange("q c t -> q (c t)"),
+                )
+        wb_grouped = keep.tile([P, H * (ND + VD), PACK], BF16, align_bytes=64)
+        wb_codes = keep.tile([P, H * (ND + VD)], U32, align_bytes=64)
+        wb_scales = keep.tile([P, H * (ND + VD)], U8, align_bytes=64)
+
+        def regroup_wb():
+            nc.scalar.copy(out=wb_grouped[:], in_=wb_raw[:].rearrange("q m n -> q n m"))
+
+        def quantise_wb():
+            nc.vector.quantize_mx(
+                out=wb_codes[:].bitcast(FP8X4),
+                scales=wb_scales[:],
+                in_=wb_grouped[:].rearrange("q n m -> q (n m)"),
+            )
+
+        x_grouped = {}
+        x_codes = {}
+        x_scales = {}
+        c_grouped = {}
+        c_codes = {}
+        c_scales = {}
+        rope_a = {}
+        rope_b = {}
+        kf_t = {}
+        v_t = {}
+
+        def transpose_unit(n):
+            x_grouped[n] = stage.tile([P, TILES * D], BF16, name="x_grouped", align_bytes=64)
+            words_in = x_sb[n][:].bitcast(F32)
+            words_out = x_grouped[n][:].bitcast(F32)
+            half = D // 2
+            for i in range(TILES):
+                xt = xt_banks.tile([P, half], F32, name="xt")
+                for b in range(half // P):
+                    nc.tensor.transpose(
+                        xt[:, b * P : (b + 1) * P],
+                        words_in[:, i * half + b * P : i * half + (b + 1) * P],
+                        ident[:],
+                    )
+                nc.scalar.copy(
+                    out=words_out[:, i * half : (i + 1) * half].rearrange(
+                        "q (g r u) -> q g r u", g=PASSES, u=2
+                    ),
+                    in_=xt[:].rearrange("q (g u r) -> q g r u", g=PASSES, u=2),
+                )
+
+        def quantise_x(n):
+            x_codes[n] = codes.tile([P, TILES * PASSES * P], U32, name="x_codes", align_bytes=64)
+            x_scales[n] = codes.tile([P, TILES * PASSES * P], U8, name="x_scales", align_bytes=64)
+            nc.vector.quantize_mx(
+                out=x_codes[n][:].bitcast(FP8X4), scales=x_scales[n][:], in_=x_grouped[n][:]
+            )
+
+        def x_cols(i, g):
+            return slice((i * PASSES + g) * P, (i * PASSES + g + 1) * P)
+
+        def rope_products(n):
+            pe = pe_banks.tile([P, TILES, 2, PAIRS], F32, name="pe")
+            for i in range(TILES):
+                for g in range(PASSES):
+                    nc.tensor.matmul_mx(
+                        out=pe[:, i].rearrange("p e j -> p (e j)"),
+                        lhsT=x_codes[n][:, x_cols(i, g)].bitcast(FP8X4),
+                        lhsT_scale=x_scales[n][:, x_cols(i, g)],
+                        rhs=wa_codes[:, g, KL:CKV].bitcast(FP8X4),
+                        rhs_scale=wa_scales[:, g, KL:CKV],
+                        start=(g == 0),
+                        stop=(g == PASSES - 1),
+                    )
+            ph = n % PHASES
+            rows = slice(ph * TILES, (ph + 1) * TILES)
+            rope_a[n] = stage.tile([P, TILES, 2, PAIRS], F32, name="rope_a")
+            rope_b[n] = stage.tile([P, TILES, 2, PAIRS], F32, name="rope_b")
+            nc.vector.tensor_tensor(
+                out=rope_a[n][:],
+                in0=pe[:],
+                in1=cos_t[:, rows, :].unsqueeze(2).to_broadcast([P, TILES, 2, PAIRS]),
+                op=ALU.mult,
+            )
+            nc.vector.scalar_tensor_tensor(
+                out=rope_b[n][:, :, 0, :],
+                in0=pe[:, :, 1, :],
+                scalar=-1.0,
+                in1=sin_t[:, rows, :],
+                op0=ALU.mult,
+                op1=ALU.mult,
+            )
+            nc.vector.tensor_tensor(
+                out=rope_b[n][:, :, 1, :], in0=pe[:, :, 0, :], in1=sin_t[:, rows, :], op=ALU.mult
+            )
+
+        def rope_finish(n):
+            kf_t[n] = results.tile([P, TILES, H, ND + RD], F32, name="kf_t")
+            nc.vector.tensor_tensor(
+                out=kf_t[n][:, :, 0, ND:].rearrange("p i (j e) -> p i j e", e=2),
+                in0=rope_a[n][:].rearrange("p i e j -> p i j e"),
+                in1=rope_b[n][:].rearrange("p i e j -> p i j e"),
+                op=ALU.add,
+            )
+            nc.vector.tensor_copy(
+                out=kf_t[n][:, :, 1:H, ND:],
+                in_=kf_t[n][:, :, 0:1, ND:].to_broadcast([P, TILES, H - 1, RD]),
+            )
+
+        def latent(n, i):
+            cb = c_banks.tile([P, PACK, P], F32, name="cb")
+            for m in range(PACK):
+                for g in range(PASSES):
+                    nc.tensor.matmul_mx(
+                        out=cb[:, m, :],
+                        lhsT=wa_codes[:, g, m * P : (m + 1) * P].bitcast(FP8X4),
+                        lhsT_scale=wa_scales[:, g, m * P : (m + 1) * P],
+                        rhs=x_codes[n][:, x_cols(i, g)].bitcast(FP8X4),
+                        rhs_scale=x_scales[n][:, x_cols(i, g)],
+                        start=(g == 0),
+                        stop=(g == PASSES - 1),
+                    )
+            c_grouped[n, i] = stage.tile([P, P, PACK], BF16, name="c_grouped%d" % i, align_bytes=64)
+            if i == 0:
+                nc.vector.tensor_copy(out=c_grouped[n, i][:], in_=cb[:].rearrange("q m r -> q r m"))
+            else:
+                nc.scalar.copy(out=c_grouped[n, i][:], in_=cb[:].rearrange("q m r -> q r m"))
+
+        def quantise_latent(n, i):
+            c_codes[n, i] = codes.tile([P, P], U32, name="c_codes%d" % i, align_bytes=64)
+            c_scales[n, i] = codes.tile([P, P], U8, name="c_scales%d" % i, align_bytes=64)
+            nc.vector.quantize_mx(
+                out=c_codes[n, i][:].bitcast(FP8X4),
+                scales=c_scales[n, i][:],
+                in_=c_grouped[n, i][:].rearrange("q r m -> q (r m)"),
+            )
+
+        def expand(n, i):
+            kv = kv_banks.tile([P, H, 2, ND], F32, name="kv")
+            nc.tensor.matmul_mx(
+                out=kv[:].rearrange("p h s d -> p (h s d)"),
+                lhsT=c_codes[n, i][:].bitcast(FP8X4),
+                lhsT_scale=c_scales[n, i][:],
+                rhs=wb_codes[:].bitcast(FP8X4),
+                rhs_scale=wb_scales[:],
+                start=True,
+                stop=True,
+            )
+            if i == 0:
+                v_t[n] = results.tile([P, TILES, H, VD], F32, name="v_t")
+            nc.scalar.copy(out=kf_t[n][:, i, :, 0:ND], in_=kv[:, :, 0, :])
+            nc.scalar.copy(out=v_t[n][:, i, :, :], in_=kv[:, :, 1, :])
+
+        def store(n):
+            nc.sync.dma_start(out=kf_units[n], in_=kf_t[n][:].rearrange("p i h f -> p (i h f)"))
+            nc.sync.dma_start(out=v_units[n], in_=v_t[n][:].rearrange("p i h f -> p (i h f)"))
+
+        def turn(n):
+            if n + 1 < UNITS:
+                transpose_unit(n + 1)
+            for i in range(TILES):
+                if n < UNITS:
+                    latent(n, i)
+                if n >= 1:
+                    expand(n - 1, i)
+            if n + 1 < UNITS:
+                quantise_x(n + 1)
+            if n < UNITS:
+                quantise_latent(n, 0)
+                rope_products(n)
+                quantise_latent(n, 1)
+                rope_finish(n)
+            if n >= 1:
+                store(n - 1)
+
+        transpose_unit(0)
+        regroup_wb()
+        quantise_x(0)
+        turn(0)
+        quantise_wb()
+        for n in range(1, UNITS + 1):
+            turn(n)

@@ -255,9 +255,13 @@ def tile_multilatentattention_pb_t_kernel(tc, x, Wkva, Wkvb, out_0, out_1):
                 in1=rope_b[n][:].rearrange("p i e j -> p i j e"),
                 op=ALU.add,
             )
-            nc.vector.tensor_copy(
+            nc.gpsimd.tensor_scalar(
                 out=kf_t[n][:, :, 1:H, ND:],
-                in_=kf_t[n][:, :, 0:1, ND:].to_broadcast([P, TILES, H - 1, RD]),
+                in0=kf_t[n][:, :, 0:1, ND:].to_broadcast([P, TILES, H - 1, RD]),
+                scalar1=1.0,
+                scalar2=0.0,
+                op0=ALU.mult,
+                op1=ALU.add,
             )
 
         def latent(n, i):

@@ -26,6 +26,7 @@ H = 4
 ND = 64
 VD = 64
 CKV = KL + RD
+KV = H * (ND + VD)
 ROPE_BASE = 10000.0
 
 TILES = 2
@@ -35,7 +36,7 @@ PHASES = SEQ // UNIT
 
 ROUND_MAGIC = 1.5 * 2.0**23
 
-FLOPS = 2 * TOKENS * D * CKV + 2 * TOKENS * KL * H * (ND + VD)
+FLOPS = 2 * TOKENS * D * CKV + 2 * TOKENS * KL * KV
 
 
 def tile_multilatentattention_pb_t_kernel(tc, x, Wkva, Wkvb, out_0, out_1):
@@ -51,35 +52,33 @@ def tile_multilatentattention_pb_t_kernel(tc, x, Wkva, Wkvb, out_0, out_1):
     with ExitStack() as ctx:
         keep = ctx.enter_context(tc.tile_pool(name="keep", bufs=1))
         x_pool = ctx.enter_context(tc.tile_pool(name="x_pool", bufs=UNITS))
-        stage = ctx.enter_context(tc.tile_pool(name="stage", bufs=2))
+        stage = ctx.enter_context(tc.tile_pool(name="stage", bufs=3))
         codes = ctx.enter_context(tc.tile_pool(name="codes", bufs=3))
-        results = ctx.enter_context(tc.tile_pool(name="results", bufs=4))
-        xt_banks = ctx.enter_context(tc.psum_pool(name="xt_banks", bufs=2))
+        results = ctx.enter_context(tc.tile_pool(name="results", bufs=8))
+        xt_banks = ctx.enter_context(tc.psum_pool(name="xt_banks", bufs=3))
         c_banks = ctx.enter_context(tc.psum_pool(name="c_banks", bufs=2))
         kv_banks = ctx.enter_context(tc.psum_pool(name="kv_banks", bufs=2))
-        pe_banks = ctx.enter_context(tc.psum_pool(name="pe_banks", bufs=2))
+        pe_banks = ctx.enter_context(tc.psum_pool(name="pe_banks", bufs=1))
         ctx.enter_context(tc.manual_schedule())
 
         wa_rows = Wkva.rearrange("(g u q e) c -> g q u (e c)", g=PASSES, u=2, q=P, e=2)
         wa_raw = keep.tile([P, PASSES, PACK, CKV], BF16)
+        for g in range(PASSES):
+            nc.sync.dma_start(
+                out=wa_raw[:, g].rearrange("q (u e) c -> q u (e c)", u=2), in_=wa_rows[g]
+            )
         x_sb = {}
 
         def load_x(n):
             x_sb[n] = x_pool.tile([P, TILES * D], BF16, name="x_sb")
             nc.sync.dma_start(out=x_sb[n][:], in_=x_units[n])
 
-        for g in range(PASSES):
-            nc.sync.dma_start(
-                out=wa_raw[:, g].rearrange("q (u e) c -> q u (e c)", u=2), in_=wa_rows[g]
-            )
         load_x(0)
-        wb_raw = keep.tile([P, PACK, H * (ND + VD)], BF16)
+        load_x(1)
+        wb_raw = keep.tile([P, PACK, KV], BF16)
         nc.sync.dma_start(out=wb_raw[:], in_=Wkvb.rearrange("(m q) n -> q m n", q=P))
-        for n in range(1, UNITS):
+        for n in range(2, UNITS):
             load_x(n)
-
-        ident = keep.tile([P, P], F32)
-        make_identity(nc, ident[:])
 
         warm = keep.tile([P, 1], F32)
         nc.vector.memset(warm[:], 0.0)
@@ -88,6 +87,8 @@ def tile_multilatentattention_pb_t_kernel(tc, x, Wkva, Wkvb, out_0, out_1):
         nc.gpsimd.iota(
             pos_i[:], pattern=[[UNIT, PHASES], [1, TILES]], base=0, channel_multiplier=TILES
         )
+        ident = keep.tile([P, P], F32)
+        make_identity(nc, ident[:])
         pos = keep.tile([P, PHASES * TILES], F32)
         nc.vector.tensor_copy(out=pos[:], in_=pos_i[:])
         turns = keep.tile([P, PAIRS], F32)
@@ -120,56 +121,42 @@ def tile_multilatentattention_pb_t_kernel(tc, x, Wkva, Wkvb, out_0, out_1):
         )
         frac = keep.tile(table_shape, F32)
         nc.vector.tensor_sub(out=frac[:], in0=angle[:], in1=whole[:])
-        frac_abs = keep.tile(table_shape, F32)
-        nc.vector.scalar_tensor_tensor(
-            out=frac_abs[:], in0=frac[:], scalar=-1.0, in1=frac[:], op0=ALU.mult, op1=ALU.max
-        )
-        quarter_off = keep.tile(table_shape, F32)
-        nc.vector.tensor_scalar(
-            out=quarter_off[:],
-            in0=frac_abs[:],
-            scalar1=-1.0,
-            scalar2=0.25,
-            op0=ALU.mult,
-            op1=ALU.add,
-        )
         sin_t = keep.tile(table_shape, F32)
+        sin_half = keep.tile(table_shape, F32)
         cos_t = keep.tile(table_shape, F32)
         nc.scalar.activation(out=sin_t[:], in_=frac[:], func=ACT.Sin, scale=2.0 * math.pi)
-        nc.scalar.activation(out=cos_t[:], in_=quarter_off[:], func=ACT.Sin, scale=2.0 * math.pi)
+        nc.scalar.activation(out=sin_half[:], in_=frac[:], func=ACT.Sin, scale=math.pi)
+        nc.scalar.activation(out=sin_half[:], in_=sin_half[:], func=ACT.Square)
+        nc.scalar.activation(out=cos_t[:], in_=sin_half[:], func=ACT.Copy, scale=-2.0, bias=1.0)
+
+        def regroup(engine_copy, grouped, raw):
+            engine_copy(
+                out=grouped.rearrange("q (c r) t -> q c t r", r=4),
+                in_=raw.rearrange("q t (c r) -> q c t r", r=4),
+            )
+
+        def quantise(words, scales, grouped):
+            nc.vector.quantize_mx(
+                out=words.bitcast(FP8X4), scales=scales, in_=grouped.rearrange("q c t -> q (c t)")
+            )
 
         wa_grouped = keep.tile([P, PASSES, CKV, PACK], BF16, align_bytes=64)
         wa_codes = keep.tile([P, PASSES, CKV], U32, align_bytes=64)
         wa_scales = keep.tile([P, PASSES, CKV], U8, align_bytes=64)
+        latent_cols = slice(0, KL)
+        rope_cols = slice(KL, CKV)
         for g in range(PASSES):
-            nc.vector.tensor_copy(
-                out=wa_grouped[:, g, 0:KL, :],
-                in_=wa_raw[:, g, :, 0:KL].rearrange("q t c -> q c t"),
-            )
+            regroup(nc.vector.tensor_copy, wa_grouped[:, g, latent_cols, :], wa_raw[:, g, :, latent_cols])
             nc.scalar.copy(
-                out=wa_grouped[:, g, KL:CKV, :].rearrange("q (e j) t -> q e j t", e=2),
-                in_=wa_raw[:, g, :, KL:CKV].rearrange("q t (j e) -> q e j t", e=2),
+                out=wa_grouped[:, g, rope_cols, :].rearrange("q (e j) t -> q e j t", e=2),
+                in_=wa_raw[:, g, :, rope_cols].rearrange("q t (j e) -> q e j t", e=2),
             )
-        for g in range(PASSES):
-            for cols in (slice(0, KL), slice(KL, CKV)):
-                nc.vector.quantize_mx(
-                    out=wa_codes[:, g, cols].bitcast(FP8X4),
-                    scales=wa_scales[:, g, cols],
-                    in_=wa_grouped[:, g, cols, :].rearrange("q c t -> q (c t)"),
-                )
-        wb_grouped = keep.tile([P, H * (ND + VD), PACK], BF16, align_bytes=64)
-        wb_codes = keep.tile([P, H * (ND + VD)], U32, align_bytes=64)
-        wb_scales = keep.tile([P, H * (ND + VD)], U8, align_bytes=64)
-
-        def regroup_wb():
-            nc.scalar.copy(out=wb_grouped[:], in_=wb_raw[:].rearrange("q m n -> q n m"))
-
-        def quantise_wb():
-            nc.vector.quantize_mx(
-                out=wb_codes[:].bitcast(FP8X4),
-                scales=wb_scales[:],
-                in_=wb_grouped[:].rearrange("q n m -> q (n m)"),
+            quantise(
+                wa_codes[:, g, latent_cols], wa_scales[:, g, latent_cols], wa_grouped[:, g, latent_cols, :]
             )
+        wb_grouped = keep.tile([P, KV, PACK], BF16, align_bytes=64)
+        wb_codes = keep.tile([P, KV], U32, align_bytes=64)
+        wb_scales = keep.tile([P, KV], U8, align_bytes=64)
 
         x_grouped = {}
         x_codes = {}
@@ -181,12 +168,12 @@ def tile_multilatentattention_pb_t_kernel(tc, x, Wkva, Wkvb, out_0, out_1):
         rope_b = {}
         kf_t = {}
         v_t = {}
+        half = D // 2
 
         def transpose_unit(n):
             x_grouped[n] = stage.tile([P, TILES * D], BF16, name="x_grouped", align_bytes=64)
             words_in = x_sb[n][:].bitcast(F32)
             words_out = x_grouped[n][:].bitcast(F32)
-            half = D // 2
             for i in range(TILES):
                 xt = xt_banks.tile([P, half], F32, name="xt")
                 for b in range(half // P):
@@ -205,9 +192,13 @@ def tile_multilatentattention_pb_t_kernel(tc, x, Wkva, Wkvb, out_0, out_1):
         def quantise_x(n):
             x_codes[n] = codes.tile([P, TILES * PASSES * P], U32, name="x_codes", align_bytes=64)
             x_scales[n] = codes.tile([P, TILES * PASSES * P], U8, name="x_scales", align_bytes=64)
-            nc.vector.quantize_mx(
-                out=x_codes[n][:].bitcast(FP8X4), scales=x_scales[n][:], in_=x_grouped[n][:]
-            )
+            for i in range(TILES):
+                cols = slice(i * PASSES * P, (i + 1) * PASSES * P)
+                nc.vector.quantize_mx(
+                    out=x_codes[n][:, cols].bitcast(FP8X4),
+                    scales=x_scales[n][:, cols],
+                    in_=x_grouped[n][:, i * D : (i + 1) * D],
+                )
 
         def x_cols(i, g):
             return slice((i * PASSES + g) * P, (i * PASSES + g + 1) * P)
@@ -220,8 +211,8 @@ def tile_multilatentattention_pb_t_kernel(tc, x, Wkva, Wkvb, out_0, out_1):
                         out=pe[:, i].rearrange("p e j -> p (e j)"),
                         lhsT=x_codes[n][:, x_cols(i, g)].bitcast(FP8X4),
                         lhsT_scale=x_scales[n][:, x_cols(i, g)],
-                        rhs=wa_codes[:, g, KL:CKV].bitcast(FP8X4),
-                        rhs_scale=wa_scales[:, g, KL:CKV],
+                        rhs=wa_codes[:, g, rope_cols].bitcast(FP8X4),
+                        rhs_scale=wa_scales[:, g, rope_cols],
                         start=(g == 0),
                         stop=(g == PASSES - 1),
                     )
@@ -286,11 +277,7 @@ def tile_multilatentattention_pb_t_kernel(tc, x, Wkva, Wkvb, out_0, out_1):
         def quantise_latent(n, i):
             c_codes[n, i] = codes.tile([P, P], U32, name="c_codes%d" % i, align_bytes=64)
             c_scales[n, i] = codes.tile([P, P], U8, name="c_scales%d" % i, align_bytes=64)
-            nc.vector.quantize_mx(
-                out=c_codes[n, i][:].bitcast(FP8X4),
-                scales=c_scales[n, i][:],
-                in_=c_grouped[n, i][:].rearrange("q r m -> q (r m)"),
-            )
+            quantise(c_codes[n, i][:], c_scales[n, i][:], c_grouped[n, i][:])
 
         def expand(n, i):
             kv = kv_banks.tile([P, H, 2, ND], F32, name="kv")
@@ -312,28 +299,35 @@ def tile_multilatentattention_pb_t_kernel(tc, x, Wkva, Wkvb, out_0, out_1):
             nc.sync.dma_start(out=kf_units[n], in_=kf_t[n][:].rearrange("p i h f -> p (i h f)"))
             nc.sync.dma_start(out=v_units[n], in_=v_t[n][:].rearrange("p i h f -> p (i h f)"))
 
+        def live(n):
+            return 0 <= n < UNITS
+
         def turn(n):
-            if n + 1 < UNITS:
-                transpose_unit(n + 1)
-            for i in range(TILES):
-                if n < UNITS:
-                    latent(n, i)
-                if n >= 1:
-                    expand(n - 1, i)
-            if n + 1 < UNITS:
+            if live(n):
+                latent(n, 0)
+                latent(n, 1)
+            if live(n + 1):
                 quantise_x(n + 1)
-            if n < UNITS:
+            if live(n):
                 quantise_latent(n, 0)
                 rope_products(n)
                 quantise_latent(n, 1)
-                rope_finish(n)
-            if n >= 1:
+            if live(n - 1):
+                expand(n - 1, 0)
+                expand(n - 1, 1)
                 store(n - 1)
+            if live(n + 2):
+                transpose_unit(n + 2)
+            if live(n):
+                rope_finish(n)
 
-        transpose_unit(0)
-        regroup_wb()
-        quantise_x(0)
+        turn(-2)
+        turn(-1)
+        for g in range(PASSES):
+            quantise(wa_codes[:, g, rope_cols], wa_scales[:, g, rope_cols], wa_grouped[:, g, rope_cols, :])
+        regroup(nc.vector.tensor_copy, wb_grouped[:, 0 : KV // 2, :], wb_raw[:, :, 0 : KV // 2])
+        regroup(nc.scalar.copy, wb_grouped[:, KV // 2 : KV, :], wb_raw[:, :, KV // 2 : KV])
         turn(0)
-        quantise_wb()
+        quantise(wb_codes[:], wb_scales[:], wb_grouped[:])
         for n in range(1, UNITS + 1):
             turn(n)

import math
from contextlib import ExitStack

import concourse.mybir as mybir
from concourse.masks import make_identity

F32 = mybir.dt.float32
BF16 = mybir.dt.bfloat16
I32 = mybir.dt.int32
U32 = mybir.dt.uint32
U8 = mybir.dt.uint8
FP8X4 = mybir.dt.float8_e4m3fn_x4
ALU = mybir.AluOpType
ACT = mybir.ActivationFunctionType

P = 128
PACK = 4
TOKENS = 4 * 1024
SEQ = 1024
D = 1024
PASSES = D // (P * PACK)
KL = 512
RD = 128
PAIRS = RD // 2
H = 4
ND = 64
VD = 64
CKV = KL + RD
KV = H * (ND + VD)
ROPE_BASE = 10000.0

TILES = 2
UNIT = TILES * P
UNITS = TOKENS // UNIT
PHASES = SEQ // UNIT

ROUND_MAGIC = 1.5 * 2.0**23

FLOPS = 2 * TOKENS * D * CKV + 2 * TOKENS * KL * KV


def tile_multilatentattention_pb_t_kernel(tc, x, Wkva, Wkvb, out_0, out_1):
    nc = tc.nc
    x_units = x.flatten_outer_dims().rearrange("(n p i) k -> n p (i k)", p=P, i=TILES)
    kf_units = out_0.rearrange("b s h f -> (b s) (h f)").rearrange(
        "(n p i) f -> n p (i f)", p=P, i=TILES
    )
    v_units = out_1.rearrange("b s h f -> (b s) (h f)").rearrange(
        "(n p i) f -> n p (i f)", p=P, i=TILES
    )

    with ExitStack() as ctx:
        keep = ctx.enter_context(tc.tile_pool(name="keep", bufs=1))
        x_pool = ctx.enter_context(tc.tile_pool(name="x_pool", bufs=UNITS))
        stage = ctx.enter_context(tc.tile_pool(name="stage", bufs=3))
        codes = ctx.enter_context(tc.tile_pool(name="codes", bufs=3))
        results = ctx.enter_context(tc.tile_pool(name="results", bufs=8))
        xt_banks = ctx.enter_context(tc.psum_pool(name="xt_banks", bufs=3))
        c_banks = ctx.enter_context(tc.psum_pool(name="c_banks", bufs=2))
        kv_banks = ctx.enter_context(tc.psum_pool(name="kv_banks", bufs=2))
        pe_banks = ctx.enter_context(tc.psum_pool(name="pe_banks", bufs=1))
        ctx.enter_context(tc.manual_schedule())

        wa_rows = Wkva.rearrange("(g u q e) c -> g q u (e c)", g=PASSES, u=2, q=P, e=2)
        wa_raw = keep.tile([P, PASSES, PACK, CKV], BF16)
        for g in range(PASSES):
            nc.sync.dma_start(
                out=wa_raw[:, g].rearrange("q (u e) c -> q u (e c)", u=2), in_=wa_rows[g]
            )
        x_sb = {}

        def load_x(n):
            x_sb[n] = x_pool.tile([P, TILES * D], BF16, name="x_sb")
            nc.sync.dma_start(out=x_sb[n][:], in_=x_units[n])

        load_x(0)
        load_x(1)
        wb_raw = keep.tile([P, PACK, KV], BF16)
        nc.sync.dma_start(out=wb_raw[:], in_=Wkvb.rearrange("(m q) n -> q m n", q=P))
        for n in range(2, UNITS):
            load_x(n)

        warm = keep.tile([P, 1], F32)
        nc.vector.memset(warm[:], 0.0)
        nc.scalar.activation(out=warm[:], in_=warm[:], func=ACT.Sin)
        pos_i = keep.tile([P, PHASES * TILES], I32)
        nc.gpsimd.iota(
            pos_i[:], pattern=[[UNIT, PHASES], [1, TILES]], base=0, channel_multiplier=TILES
        )
        ident = keep.tile([P, P], F32)
        make_identity(nc, ident[:])
        pos = keep.tile([P, PHASES * TILES], F32)
        nc.vector.tensor_copy(out=pos[:], in_=pos_i[:])
        turns = keep.tile([P, PAIRS], F32)
        nc.vector.memset(turns[:, 0:1], 1.0)
        nc.vector.tensor_scalar_mul(out=turns[:, 0:1], in0=turns[:, 0:1], scalar1=0.5 / math.pi)
        filled = 1
        while filled < PAIRS:
            nc.vector.tensor_scalar_mul(
                out=turns[:, filled : 2 * filled],
                in0=turns[:, 0:filled],
                scalar1=ROPE_BASE ** (-2.0 * filled / RD),
            )
            filled *= 2
        table_shape = [P, PHASES * TILES, PAIRS]
        angle = keep.tile(table_shape, F32)
        nc.vector.tensor_tensor(
            out=angle[:],
            in0=pos[:].unsqueeze(2).to_broadcast(table_shape),
            in1=turns[:].unsqueeze(1).to_broadcast(table_shape),
            op=ALU.mult,
        )
        whole = keep.tile(table_shape, F32)
        nc.vector.tensor_scalar(
            out=whole[:],
            in0=angle[:],
            scalar1=ROUND_MAGIC,
            scalar2=ROUND_MAGIC,
            op0=ALU.add,
            op1=ALU.subtract,
        )
        frac = keep.tile(table_shape, F32)
        nc.vector.tensor_sub(out=frac[:], in0=angle[:], in1=whole[:])
        sin_t = keep.tile(table_shape, F32)
        sin_half = keep.tile(table_shape, F32)
        cos_t = keep.tile(table_shape, F32)
        nc.scalar.activation(out=sin_t[:], in_=frac[:], func=ACT.Sin, scale=2.0 * math.pi)
        nc.scalar.activation(out=sin_half[:], in_=frac[:], func=ACT.Sin, scale=math.pi)
        nc.scalar.activation(out=sin_half[:], in_=sin_half[:], func=ACT.Square)
        nc.scalar.activation(out=cos_t[:], in_=sin_half[:], func=ACT.Copy, scale=-2.0, bias=1.0)

        def regroup(engine_copy, grouped, raw):
            engine_copy(
                out=grouped.rearrange("q (c r) t -> q c t r", r=4),
                in_=raw.rearrange("q t (c r) -> q c t r", r=4),
            )

        def quantise(words, scales, grouped):
            nc.vector.quantize_mx(
                out=words.bitcast(FP8X4), scales=scales, in_=grouped.rearrange("q c t -> q (c t)")
            )

        wa_grouped = keep.tile([P, PASSES, CKV, PACK], BF16, align_bytes=64)
        wa_codes = keep.tile([P, PASSES, CKV], U32, align_bytes=64)
        wa_scales = keep.tile([P, PASSES, CKV], U8, align_bytes=64)
        latent_cols = slice(0, KL)
        rope_cols = slice(KL, CKV)
        for g in range(PASSES):
            regroup(nc.vector.tensor_copy, wa_grouped[:, g, latent_cols, :], wa_raw[:, g, :, latent_cols])
            nc.scalar.copy(
                out=wa_grouped[:, g, rope_cols, :].rearrange("q (e j) t -> q e j t", e=2),
                in_=wa_raw[:, g, :, rope_cols].rearrange("q t (j e) -> q e j t", e=2),
            )
            quantise(
                wa_codes[:, g, latent_cols], wa_scales[:, g, latent_cols], wa_grouped[:, g, latent_cols, :]
            )
        wb_grouped = keep.tile([P, KV, PACK], BF16, align_bytes=64)
        wb_codes = keep.tile([P, KV], U32, align_bytes=64)
        wb_scales = keep.tile([P, KV], U8, align_bytes=64)

        x_grouped = {}
        x_codes = {}
        x_scales = {}
        c_grouped = {}
        c_codes = {}
        c_scales = {}
        rope_a = {}
        rope_b = {}
        kf_t = {}
        v_t = {}
        half = D // 2

        def transpose_unit(n):
            x_grouped[n] = stage.tile([P, TILES * D], BF16, name="x_grouped", align_bytes=64)
            words_in = x_sb[n][:].bitcast(F32)
            words_out = x_grouped[n][:].bitcast(F32)
            for i in range(TILES):
                xt = xt_banks.tile([P, half], F32, name="xt")
                for b in range(half // P):
                    nc.tensor.transpose(
                        xt[:, b * P : (b + 1) * P],
                        words_in[:, i * half + b * P : i * half + (b + 1) * P],
                        ident[:],
                    )
                nc.scalar.copy(
                    out=words_out[:, i * half : (i + 1) * half].rearrange(
                        "q (g r u) -> q g r u", g=PASSES, u=2
                    ),
                    in_=xt[:].rearrange("q (g u r) -> q g r u", g=PASSES, u=2),
                )

        def quantise_x(n):
            x_codes[n] = codes.tile([P, TILES * PASSES * P], U32, name="x_codes", align_bytes=64)
            x_scales[n] = codes.tile([P, TILES * PASSES * P], U8, name="x_scales", align_bytes=64)
            for i in range(TILES):
                cols = slice(i * PASSES * P, (i + 1) * PASSES * P)
                nc.vector.quantize_mx(
                    out=x_codes[n][:, cols].bitcast(FP8X4),
                    scales=x_scales[n][:, cols],
                    in_=x_grouped[n][:, i * D : (i + 1) * D],
                )

        def x_cols(i, g):
            return slice((i * PASSES + g) * P, (i * PASSES + g + 1) * P)

        def rope_products(n):
            pe = pe_banks.tile([P, TILES, 2, PAIRS], F32, name="pe")
            for i in range(TILES):
                for g in range(PASSES):
                    nc.tensor.matmul_mx(
                        out=pe[:, i].rearrange("p e j -> p (e j)"),
                        lhsT=x_codes[n][:, x_cols(i, g)].bitcast(FP8X4),
                        lhsT_scale=x_scales[n][:, x_cols(i, g)],
                        rhs=wa_codes[:, g, rope_cols].bitcast(FP8X4),
                        rhs_scale=wa_scales[:, g, rope_cols],
                        start=(g == 0),
                        stop=(g == PASSES - 1),
                    )
            ph = n % PHASES
            rows = slice(ph * TILES, (ph + 1) * TILES)
            rope_a[n] = stage.tile([P, TILES, 2, PAIRS], F32, name="rope_a")
            rope_b[n] = stage.tile([P, TILES, 2, PAIRS], F32, name="rope_b")
            nc.vector.tensor_tensor(
                out=rope_a[n][:],
                in0=pe[:],
                in1=cos_t[:, rows, :].unsqueeze(2).to_broadcast([P, TILES, 2, PAIRS]),
                op=ALU.mult,
            )
            nc.vector.scalar_tensor_tensor(
                out=rope_b[n][:, :, 0, :],
                in0=pe[:, :, 1, :],
                scalar=-1.0,
                in1=sin_t[:, rows, :],
                op0=ALU.mult,
                op1=ALU.mult,
            )
            nc.vector.tensor_tensor(
                out=rope_b[n][:, :, 1, :], in0=pe[:, :, 0, :], in1=sin_t[:, rows, :], op=ALU.mult
            )

        def rope_finish(n):
            kf_t[n] = results.tile([P, TILES, H, ND + RD], F32, name="kf_t")
            nc.vector.tensor_tensor(
                out=kf_t[n][:, :, 0, ND:].rearrange("p i (j e) -> p i j e", e=2),
                in0=rope_a[n][:].rearrange("p i e j -> p i j e"),
                in1=rope_b[n][:].rearrange("p i e j -> p i j e"),
                op=ALU.add,
            )
            nc.gpsimd.tensor_scalar(
                out=kf_t[n][:, :, 1:H, ND:],
                in0=kf_t[n][:, :, 0:1, ND:].to_broadcast([P, TILES, H - 1, RD]),
                scalar1=1.0,
                scalar2=0.0,
                op0=ALU.mult,
                op1=ALU.add,
            )

        def latent(n, i):
            cb = c_banks.tile([P, PACK, P], F32, name="cb")
            for m in range(PACK):
                for g in range(PASSES):
                    nc.tensor.matmul_mx(
                        out=cb[:, m, :],
                        lhsT=wa_codes[:, g, m * P : (m + 1) * P].bitcast(FP8X4),
                        lhsT_scale=wa_scales[:, g, m * P : (m + 1) * P],
                        rhs=x_codes[n][:, x_cols(i, g)].bitcast(FP8X4),
                        rhs_scale=x_scales[n][:, x_cols(i, g)],
                        start=(g == 0),
                        stop=(g == PASSES - 1),
                    )
            c_grouped[n, i] = stage.tile([P, P, PACK], BF16, name="c_grouped%d" % i, align_bytes=64)
            if i == 0:
                nc.vector.tensor_copy(out=c_grouped[n, i][:], in_=cb[:].rearrange("q m r -> q r m"))
            else:
                nc.scalar.copy(out=c_grouped[n, i][:], in_=cb[:].rearrange("q m r -> q r m"))

        def quantise_latent(n, i):
            c_codes[n, i] = codes.tile([P, P], U32, name="c_codes%d" % i, align_bytes=64)
            c_scales[n, i] = codes.tile([P, P], U8, name="c_scales%d" % i, align_bytes=64)
            quantise(c_codes[n, i][:], c_scales[n, i][:], c_grouped[n, i][:])

        def expand(n, i):
            kv = kv_banks.tile([P, H, 2, ND], F32, name="kv")
            nc.tensor.matmul_mx(
                out=kv[:].rearrange("p h s d -> p (h s d)"),
                lhsT=c_codes[n, i][:].bitcast(FP8X4),
                lhsT_scale=c_scales[n, i][:],
                rhs=wb_codes[:].bitcast(FP8X4),
                rhs_scale=wb_scales[:],
                start=True,
                stop=True,
            )
            if i == 0:
                v_t[n] = results.tile([P, TILES, H, VD], F32, name="v_t")
            nc.scalar.copy(out=kf_t[n][:, i, :, 0:ND], in_=kv[:, :, 0, :])
            nc.scalar.copy(out=v_t[n][:, i, :, :], in_=kv[:, :, 1, :])

        def store(n):
            nc.sync.dma_start(out=kf_units[n], in_=kf_t[n][:].rearrange("p i h f -> p (i h f)"))
            nc.sync.dma_start(out=v_units[n], in_=v_t[n][:].rearrange("p i h f -> p (i h f)"))

        def live(n):
            return 0 <= n < UNITS

        def turn(n):
            if live(n):
                latent(n, 0)
                latent(n, 1)
            if live(n + 1):
                quantise_x(n + 1)
            if live(n):
                quantise_latent(n, 0)
                rope_products(n)
                quantise_latent(n, 1)
            if live(n - 1):
                expand(n - 1, 0)
                expand(n - 1, 1)
                store(n - 1)
            if live(n + 2):
                transpose_unit(n + 2)
            if live(n):
                rope_finish(n)

        turn(-2)
        turn(-1)
        for g in range(PASSES):
            quantise(wa_codes[:, g, rope_cols], wa_scales[:, g, rope_cols], wa_grouped[:, g, rope_cols, :])
        regroup(nc.vector.tensor_copy, wb_grouped[:, 0 : KV // 2, :], wb_raw[:, :, 0 : KV // 2])
        regroup(nc.scalar.copy, wb_grouped[:, KV // 2 : KV, :], wb_raw[:, :, KV // 2 : KV])
        turn(0)
        quantise(wb_codes[:], wb_scales[:], wb_grouped[:])
        for n in range(1, UNITS + 1):
            turn(n)
